import numpy as np
import ml_dtypes


def mxq(x, axis, fmt="e4m3"):
    dtype, down = {"e4m3": (ml_dtypes.float8_e4m3fn, 7), "e5m2": (ml_dtypes.float8_e5m2, 14)}[fmt]
    v = np.moveaxis(np.asarray(x, np.float32).astype(ml_dtypes.bfloat16).astype(np.float64), axis, -1)
    blocks = v.reshape(v.shape[:-1] + (-1, 32))
    amax = np.abs(blocks).max(-1, keepdims=True)
    byte = np.maximum(np.where(amax > 0, np.frexp(amax)[1] - 1 + 127, 0) - down, 1)
    scale = np.exp2(byte - 127.0)
    codes = (blocks / scale).astype(np.float32).astype(dtype).astype(np.float64)
    return np.moveaxis((codes * scale).reshape(v.shape), -1, axis)


WIDE = False


def mx_kscale(k):
    if not WIDE:
        return np.ones(k)
    levels = np.array([10, -10, 5, -5, 0])
    a = np.random.permutation(np.resize(levels, k // 512 * 4)).reshape(k // 512, 4)
    idx = np.arange(k)
    return np.exp2(a[idx // 512, idx % 128 // 32])


BF16 = ml_dtypes.bfloat16


def bf(x):
    return np.asarray(x, np.float32).astype(BF16)


def f64(x):
    return np.asarray(x).astype(np.float64)


E2M1 = np.array([0.0, 0.5, 1.0, 1.5, 2.0, 3.0, 4.0, 6.0, -0.0, -0.5, -1.0, -1.5, -2.0, -3.0, -4.0, -6.0])


def pack_weight(w, fmt):
    k, n = w.shape
    w = f64(bf(w)).reshape(k // 32, 32, n)
    amax = np.abs(w).max(1)
    if fmt == "e4m3":
        byte = np.frexp(amax)[1] - 1 + 127 - 7
    else:
        mant, ex = np.frexp(amax / 6.0)
        byte = np.where(mant > 0.5, ex, ex - 1) + 127
    byte = np.clip(np.where(amax > 0, byte, 1), 1, 254)
    scaled = (w * np.exp2(127.0 - byte)[:, None, :]).reshape(k, n).astype(np.float32)
    by_word = np.ascontiguousarray(scaled.reshape(k // 512, 128, 4, n).transpose(0, 1, 3, 2))
    if fmt == "e4m3":
        words = by_word.astype(ml_dtypes.float8_e4m3fn).view(np.uint8)
    else:
        c = by_word.astype(ml_dtypes.float4_e2m1fn).view(np.uint8) & 0xF
        words = c[..., 0::2] | (c[..., 1::2] << 4)
    return np.ascontiguousarray(words), np.ascontiguousarray(byte.astype(np.uint8).reshape(k // 512, 16, n))


def unpack_weight(words, scales, fmt):
    g, p, n, _ = words.shape
    if fmt == "e4m3":
        vals = np.ascontiguousarray(words).view(ml_dtypes.float8_e4m3fn).astype(np.float64)
    else:
        nib = np.empty((g, p, n, 4), np.uint8)
        nib[..., 0::2] = words & 0xF
        nib[..., 1::2] = words >> 4
        vals = E2M1[nib]
    vals = vals * np.repeat(np.exp2(scales.astype(np.float64) - 127.0), 8, axis=1)[..., None]
    return vals.transpose(0, 1, 3, 2).reshape(g * 512, n)

def pack4(w):
    words, scales = pack_weight(w, "e2m1")
    return words.reshape(words.shape[0], 128, -1), scales


def unpack4(words, scales):
    return unpack_weight(words.reshape(words.shape[0], 128, -1, 2), scales, "e2m1")


B, IN, H = 512, 512, 1024


def sigmoid(v):
    return 1.0 / (1.0 + np.exp(-v))


def setup_inputs():
    s = mx_kscale(IN)
    g = np.random.standard_normal((H, IN + H)) / np.sqrt(IN + H)
    g[:, :IN] /= s
    x = bf(np.random.standard_normal((B, IN)) * s)
    h = bf(np.random.standard_normal((B, H)))
    tau = bf(np.random.standard_normal(H))
    w_in = np.random.standard_normal((H, IN)) / np.sqrt(IN) / s
    w_rec = np.random.standard_normal((H, H)) * 1.5 / np.sqrt(H)
    gate_b = bf(np.random.standard_normal(H) * 0.5)
    W_in_words, W_in_scales = pack4(np.ascontiguousarray(w_in.T))
    W_rec_words, W_rec_scales = pack4(np.ascontiguousarray(w_rec.T))
    gate_w_words, gate_w_scales = pack4(np.ascontiguousarray(g.T))
    return {"x": x,
            "h": h,
            "tau": tau,
            "W_in_words": W_in_words,
            "W_in_scales": W_in_scales,
            "W_rec_words": W_rec_words,
            "W_rec_scales": W_rec_scales,
            "gate_w_words": gate_w_words,
            "gate_w_scales": gate_w_scales,
            "gate_b": gate_b}


def reference(x, h, tau, W_in_words, W_in_scales, W_rec_words, W_rec_scales, gate_w_words, gate_w_scales, gate_b):
    tau_p = np.log(1.0 + np.exp(f64(tau))) + 1.0
    gt = unpack4(gate_w_words, gate_w_scales)
    xq = mxq(f64(x), 1, "e4m3")
    hq = mxq(f64(h), 1, "e4m3")
    x_in = xq @ unpack4(W_in_words, W_in_scales)
    pre = (xq @ gt[:IN]) + (hq @ gt[IN:]) + f64(gate_b)
    gate = sigmoid(np.tanh(pre))
    k1 = -f64(h) / tau_p + x_in + gate * (hq @ unpack4(W_rec_words, W_rec_scales))
    return x_in, k1

@@ -1,0 +1,225 @@
+from contextlib import ExitStack
+
+import concourse.mybir as mybir
+from concourse.masks import make_identity
+
+F32 = mybir.dt.float32
+BF16 = mybir.dt.bfloat16
+U8 = mybir.dt.uint8
+U32 = mybir.dt.uint32
+I32 = mybir.dt.int32
+FP8X4 = mybir.dt.float8_e4m3fn_x4
+FP4X4 = mybir.dt.float4_e2m1fn_x4
+ACT = mybir.ActivationFunctionType
+ALU = mybir.AluOpType
+
+P = 128
+B, IN, H = 512, 512, 1024
+K_PASS = 512
+WORDS = K_PASS // 2
+N_TILE = 512
+TOKEN_TILES = B // P
+HALVES = H // N_TILE
+CHUNKS = H // P
+
+W_IN, GATE, W_REC = 0, 1, 4
+W_PASSES = 6
+X_PASS, H_PASS = 0, 1
+A_PASSES = 3
+
+INV_E = 0.36787944117144233
+
+FLOPS = 2 * B * H * (IN + (IN + H) + H)
+
+
+def tile_ltccell_pa_kernel(
+    tc,
+    x,
+    h,
+    tau,
+    W_in_words,
+    W_in_scales,
+    W_rec_words,
+    W_rec_scales,
+    gate_w_words,
+    gate_w_scales,
+    gate_b,
+    out_0,
+    out_1,
+):
+    nc = tc.nc
+    with ExitStack() as ctx:
+        keep = ctx.enter_context(tc.tile_pool(name="keep", bufs=1))
+        stage = ctx.enter_context(tc.tile_pool(name="stage", bufs=2))
+        ahead = ctx.enter_context(tc.tile_pool(name="ahead", bufs=TOKEN_TILES * HALVES))
+        work = ctx.enter_context(tc.tile_pool(name="work", bufs=3))
+        psum = ctx.enter_context(tc.psum_pool(name="psum", bufs=2))
+
+        ident = keep.tile([P, P], F32)
+        vec_rows = keep.tile([P, P], BF16)
+        x_sb = keep.tile([P, TOKEN_TILES, IN], BF16)
+        h_sb = keep.tile([P, TOKEN_TILES, H], BF16)
+        w_words = keep.tile([P, W_PASSES, 2 * H], U8, align_bytes=64)
+        w_scales = keep.tile([P, W_PASSES, H], U8, align_bytes=64)
+        a_words = keep.tile([P, TOKEN_TILES, A_PASSES, P], U32, align_bytes=64)
+        a_scales = keep.tile([P, TOKEN_TILES, A_PASSES, P], U8, align_bytes=64)
+        bias_all = keep.tile([P, H], F32)
+        inv_tau_all = keep.tile([P, H], F32)
+
+        make_identity(nc, ident[:])
+        nc.vector.memset(vec_rows[:], 0.0)
+        nc.vector.memset(w_scales[:].bitcast(I32), 0)
+
+        def load_tokens(t):
+            rows = slice(t * P, (t + 1) * P)
+            nc.sync.dma_start(out=x_sb[:, t, :], in_=x[rows, :])
+            nc.sync.dma_start(out=h_sb[:, t, :], in_=h[rows, :])
+
+        def load_scales(scales, first):
+            passes = scales.shape[0]
+            for quad in range(4):
+                nc.sync.dma_start(
+                    out=w_scales[32 * quad : 32 * quad + 4, first : first + passes, :].bitcast(I32),
+                    in_=scales[:, 4 * quad : 4 * quad + 4, :].rearrange("g r n -> r g n").bitcast(I32),
+                )
+
+        def load_words(words, first, half):
+            passes = words.shape[0]
+            cols = slice(half * 2 * N_TILE, (half + 1) * 2 * N_TILE)
+            nc.sync.dma_start(
+                out=w_words[:, first : first + passes, cols].bitcast(I32),
+                in_=words[:, :, cols].rearrange("g p b -> p g b").bitcast(I32),
+            )
+
+        nc.sync.dma_start(out=vec_rows[0:CHUNKS, :], in_=tau.rearrange("(j c) -> j c", c=P))
+        nc.sync.dma_start(out=vec_rows[CHUNKS : 2 * CHUNKS, :], in_=gate_b.rearrange("(j c) -> j c", c=P))
+        load_tokens(0)
+        load_scales(W_in_scales, W_IN)
+        load_scales(gate_w_scales, GATE)
+        load_scales(W_rec_scales, W_REC)
+        load_words(W_in_words, W_IN, 0)
+        load_words(gate_w_words, GATE, 0)
+        load_words(W_rec_words, W_REC, 0)
+        for t in range(1, TOKEN_TILES):
+            load_tokens(t)
+        load_words(W_in_words, W_IN, 1)
+        load_words(gate_w_words, GATE, 1)
+        load_words(W_rec_words, W_REC, 1)
+
+        vec_f32 = keep.tile([P, P], F32)
+        nc.vector.tensor_copy(out=vec_f32[:], in_=vec_rows[:])
+        vec_t = psum.tile([P, P], F32, tag="turn")
+        nc.tensor.transpose(vec_t[:], vec_f32[:], ident[:])
+        vec_cols = keep.tile([P, 2 * CHUNKS], F32)
+        nc.vector.tensor_copy(out=vec_cols[:], in_=vec_t[:, 0 : 2 * CHUNKS])
+        tau_cols = vec_cols[:, 0:CHUNKS]
+        bias_cols = vec_cols[:, CHUNKS : 2 * CHUNKS]
+
+        tau_abs = keep.tile([P, CHUNKS], F32)
+        nc.vector.scalar_tensor_tensor(
+            out=tau_abs[:], in0=tau_cols, scalar=-1.0, in1=tau_cols, op0=ALU.mult, op1=ALU.max
+        )
+        tau_sig = keep.tile([P, CHUNKS], F32)
+        nc.scalar.activation(out=tau_sig[:], in_=tau_abs[:], func=ACT.Sigmoid)
+        tau_log = keep.tile([P, CHUNKS], F32)
+        nc.scalar.activation(out=tau_log[:], in_=tau_sig[:], func=ACT.Ln, scale=INV_E)
+        tau_p = keep.tile([P, CHUNKS], F32)
+        nc.vector.scalar_tensor_tensor(
+            out=tau_p[:], in0=tau_cols, scalar=0.0, in1=tau_log[:], op0=ALU.max, op1=ALU.subtract
+        )
+        inv_tau_cols = keep.tile([P, CHUNKS], F32)
+        nc.vector.reciprocal(out=inv_tau_cols[:], in_=tau_p[:])
+
+        def spread(one_to_a_partition, everywhere):
+            for half in range(HALVES):
+                bank = psum.tile([P, N_TILE], F32, tag="turn")
+                for q in range(N_TILE // P):
+                    j = half * (N_TILE // P) + q
+                    nc.tensor.transpose(
+                        bank[:, q * P : (q + 1) * P], one_to_a_partition[:, j : j + 1].to_broadcast([P, P]), ident[:]
+                    )
+                nc.vector.tensor_copy(out=everywhere[:, half * N_TILE : (half + 1) * N_TILE], in_=bank[:])
+
+        def turn(words, passes):
+            turned = psum.tile([P, passes, 2, P], F32, tag="turn")
+            for g in range(passes):
+                for u in range(2):
+                    nc.tensor.transpose(
+                        turned[:, g, u, :], words[:, WORDS * g + u : WORDS * (g + 1) : 2], ident[:]
+                    )
+            return turned
+
+        def quantise(t, first, passes, grouped):
+            chosen = slice(first, first + passes)
+            nc.vector.quantize_mx(
+                out=a_words[:, t, chosen, :].rearrange("p g r -> p (g r)").bitcast(FP8X4),
+                scales=a_scales[:, t, chosen, :].rearrange("p g r -> p (g r)"),
+                in_=grouped[:, chosen, :].rearrange("p g c -> p (g c)"),
+            )
+
+        def prepare(t):
+            x_turned = turn(x_sb[:, t, :].bitcast(F32), 1)
+            h_turned = turn(h_sb[:, t, :].bitcast(F32), 2)
+            grouped = stage.tile([P, A_PASSES, 4 * P], BF16, align_bytes=64)
+            word_halves = grouped[:].bitcast(F32).rearrange("p g (r u) -> p g r u", u=2)
+            nc.vector.tensor_copy(
+                out=word_halves[:, X_PASS : X_PASS + 1], in_=x_turned[:].rearrange("p g u r -> p g r u")
+            )
+            nc.scalar.copy(out=word_halves[:, H_PASS : H_PASS + 2], in_=h_turned[:].rearrange("p g u r -> p g r u"))
+            quantise(t, X_PASS, 1, grouped)
+            quantise(t, H_PASS, 2, grouped)
+
+        def mx_sum(acc, t, half, operands):
+            cols = slice(half * N_TILE, (half + 1) * N_TILE)
+            byte_cols = slice(half * 2 * N_TILE, (half + 1) * 2 * N_TILE)
+            for i, (a, w) in enumerate(operands):
+                nc.tensor.matmul_mx(
+                    out=acc[:],
+                    lhsT=a_words[:, t, a, :].bitcast(FP8X4),
+                    lhsT_scale=a_scales[:, t, a, :],
+                    rhs=w_words[:, w, byte_cols].bitcast(FP4X4),
+                    rhs_scale=w_scales[:, w, cols],
+                    start=(i == 0),
+                    stop=(i == len(operands) - 1),
+                )
+
+        def output_tile(t, half):
+            rows = slice(t * P, (t + 1) * P)
+            cols = slice(half * N_TILE, (half + 1) * N_TILE)
+
+            x_in_acc = psum.tile([P, N_TILE], F32, tag="x_in")
+            mx_sum(x_in_acc, t, half, [(X_PASS, W_IN)])
+            pre_acc = psum.tile([P, N_TILE], F32, tag="pre")
+            mx_sum(pre_acc, t, half, [(X_PASS, GATE), (H_PASS, GATE + 1), (H_PASS + 1, GATE + 2)])
+            rec_acc = psum.tile([P, N_TILE], F32, tag="rec")
+            mx_sum(rec_acc, t, half, [(H_PASS, W_REC), (H_PASS + 1, W_REC + 1)])
+
+            x_in = work.tile([P, N_TILE], F32)
+            nc.scalar.copy(out=x_in[:], in_=x_in_acc[:])
+            nc.sync.dma_start(out=out_0[rows, cols], in_=x_in[:])
+
+            leak = ahead.tile([P, N_TILE], F32)
+            nc.gpsimd.tensor_tensor(out=leak[:], in0=h_sb[:, t, cols], in1=inv_tau_all[:, cols], op=ALU.mult)
+            base = work.tile([P, N_TILE], F32)
+            nc.gpsimd.tensor_tensor(out=base[:], in0=x_in[:], in1=leak[:], op=ALU.subtract)
+
+            pre = work.tile([P, N_TILE], F32)
+            nc.vector.tensor_tensor(out=pre[:], in0=pre_acc[:], in1=bias_all[:, cols], op=ALU.add)
+            squashed = work.tile([P, N_TILE], F32)
+            nc.scalar.activation(out=squashed[:], in_=pre[:], func=ACT.Tanh)
+            gate = work.tile([P, N_TILE], F32)
+            nc.scalar.activation(out=gate[:], in_=squashed[:], func=ACT.Sigmoid)
+            gated = work.tile([P, N_TILE], F32)
+            nc.vector.tensor_tensor(out=gated[:], in0=gate[:], in1=rec_acc[:], op=ALU.mult)
+            k1 = work.tile([P, N_TILE], F32)
+            nc.vector.tensor_tensor(out=k1[:], in0=gated[:], in1=base[:], op=ALU.add)
+            nc.sync.dma_start(out=out_1[rows, cols], in_=k1[:])
+
+        prepare(0)
+        spread(bias_cols, bias_all)
+        spread(inv_tau_cols, inv_tau_all)
+        for half in range(HALVES):
+            for t in range(TOKEN_TILES):
+                if half == 0 and t + 1 < TOKEN_TILES:
+                    prepare(t + 1)
+                output_tile(t, half)

@@ -24,8 +24,6 @@ CHUNKS = H // P
 
 W_IN, GATE, W_REC = 0, 1, 4
 W_PASSES = 6
-X_PASS, H_PASS = 0, 1
-A_PASSES = 3
 
 INV_E = 0.36787944117144233
 
@@ -50,10 +48,8 @@ def tile_ltccell_pa_kernel(
     nc = tc.nc
     with ExitStack() as ctx:
         keep = ctx.enter_context(tc.tile_pool(name="keep", bufs=1))
-        stage = ctx.enter_context(tc.tile_pool(name="stage", bufs=2))
-        ahead = ctx.enter_context(tc.tile_pool(name="ahead", bufs=TOKEN_TILES * HALVES))
-        work = ctx.enter_context(tc.tile_pool(name="work", bufs=3))
-        psum = ctx.enter_context(tc.psum_pool(name="psum", bufs=2))
+        work = ctx.enter_context(tc.tile_pool(name="work", bufs=4))
+        psum = ctx.enter_context(tc.psum_pool(name="psum", bufs=8))
 
         ident = keep.tile([P, P], F32)
         vec_rows = keep.tile([P, P], BF16)
@@ -61,54 +57,52 @@ def tile_ltccell_pa_kernel(
         h_sb = keep.tile([P, TOKEN_TILES, H], BF16)
         w_words = keep.tile([P, W_PASSES, 2 * H], U8, align_bytes=64)
         w_scales = keep.tile([P, W_PASSES, H], U8, align_bytes=64)
-        a_words = keep.tile([P, TOKEN_TILES, A_PASSES, P], U32, align_bytes=64)
-        a_scales = keep.tile([P, TOKEN_TILES, A_PASSES, P], U8, align_bytes=64)
+        x_grouped = keep.tile([P, TOKEN_TILES, 4 * P], BF16, align_bytes=64)
+        x_words = keep.tile([P, TOKEN_TILES, P], U32, align_bytes=64)
+        x_scales = keep.tile([P, TOKEN_TILES, P], U8, align_bytes=64)
+        h_grouped = keep.tile([P, 2 * TOKEN_TILES, 4 * P], BF16, align_bytes=64)
+        h_words = keep.tile([P, 2 * TOKEN_TILES, P], U32, align_bytes=64)
+        h_scales = keep.tile([P, 2 * TOKEN_TILES, P], U8, align_bytes=64)
         bias_all = keep.tile([P, H], F32)
         inv_tau_all = keep.tile([P, H], F32)
+        leak = keep.tile([P, TOKEN_TILES, H], F32)
 
         make_identity(nc, ident[:])
         nc.vector.memset(vec_rows[:], 0.0)
         nc.vector.memset(w_scales[:].bitcast(I32), 0)
 
-        def load_tokens(t):
-            rows = slice(t * P, (t + 1) * P)
-            nc.sync.dma_start(out=x_sb[:, t, :], in_=x[rows, :])
-            nc.sync.dma_start(out=h_sb[:, t, :], in_=h[rows, :])
-
         def load_scales(scales, first):
             passes = scales.shape[0]
-            for quad in range(4):
+            for r in range(4):
                 nc.sync.dma_start(
-                    out=w_scales[32 * quad : 32 * quad + 4, first : first + passes, :].bitcast(I32),
-                    in_=scales[:, 4 * quad : 4 * quad + 4, :].rearrange("g r n -> r g n").bitcast(I32),
+                    out=w_scales[r:P:32, first : first + passes, :].bitcast(I32),
+                    in_=scales[:, r:16:4, :].rearrange("g q n -> q g n").bitcast(I32),
                 )
 
         def load_words(words, first, half):
             passes = words.shape[0]
-            cols = slice(half * 2 * N_TILE, (half + 1) * 2 * N_TILE)
+            byte_cols = slice(half * 2 * N_TILE, (half + 1) * 2 * N_TILE)
             nc.sync.dma_start(
-                out=w_words[:, first : first + passes, cols].bitcast(I32),
-                in_=words[:, :, cols].rearrange("g p b -> p g b").bitcast(I32),
+                out=w_words[:, first : first + passes, byte_cols].bitcast(I32),
+                in_=words[:, :, byte_cols].rearrange("g p b -> p g b").bitcast(I32),
             )
 
         nc.sync.dma_start(out=vec_rows[0:CHUNKS, :], in_=tau.rearrange("(j c) -> j c", c=P))
         nc.sync.dma_start(out=vec_rows[CHUNKS : 2 * CHUNKS, :], in_=gate_b.rearrange("(j c) -> j c", c=P))
-        load_tokens(0)
-        load_scales(W_in_scales, W_IN)
+        nc.sync.dma_start(out=x_sb[:], in_=x.rearrange("(t p) k -> p t k", p=P))
+        nc.sync.dma_start(out=h_sb[:, 0:2, :], in_=h[0 : 2 * P, :].rearrange("(t p) k -> p t k", p=P))
+        nc.sync.dma_start(out=h_sb[:, 2:4, :], in_=h[2 * P : 4 * P, :].rearrange("(t p) k -> p t k", p=P))
         load_scales(gate_w_scales, GATE)
+        load_scales(W_in_scales, W_IN)
         load_scales(W_rec_scales, W_REC)
-        load_words(W_in_words, W_IN, 0)
-        load_words(gate_w_words, GATE, 0)
-        load_words(W_rec_words, W_REC, 0)
-        for t in range(1, TOKEN_TILES):
-            load_tokens(t)
-        load_words(W_in_words, W_IN, 1)
-        load_words(gate_w_words, GATE, 1)
-        load_words(W_rec_words, W_REC, 1)
+        for half in range(HALVES):
+            load_words(gate_w_words, GATE, half)
+            load_words(W_in_words, W_IN, half)
+            load_words(W_rec_words, W_REC, half)
 
         vec_f32 = keep.tile([P, P], F32)
         nc.vector.tensor_copy(out=vec_f32[:], in_=vec_rows[:])
-        vec_t = psum.tile([P, P], F32, tag="turn")
+        vec_t = psum.tile([P, P], F32, tag="bank")
         nc.tensor.transpose(vec_t[:], vec_f32[:], ident[:])
         vec_cols = keep.tile([P, 2 * CHUNKS], F32)
         nc.vector.tensor_copy(out=vec_cols[:], in_=vec_t[:, 0 : 2 * CHUNKS])
@@ -132,94 +126,105 @@ def tile_ltccell_pa_kernel(
 
         def spread(one_to_a_partition, everywhere):
             for half in range(HALVES):
-                bank = psum.tile([P, N_TILE], F32, tag="turn")
+                bank = psum.tile([P, N_TILE], F32, tag="bank")
                 for q in range(N_TILE // P):
                     j = half * (N_TILE // P) + q
                     nc.tensor.transpose(
-                        bank[:, q * P : (q + 1) * P], one_to_a_partition[:, j : j + 1].to_broadcast([P, P]), ident[:]
+                        bank[:, q * P : (q + 1) * P],
+                        one_to_a_partition[:, j : j + 1].to_broadcast([P, P]),
+                        ident[:],
                     )
                 nc.vector.tensor_copy(out=everywhere[:, half * N_TILE : (half + 1) * N_TILE], in_=bank[:])
 
-        def turn(words, passes):
-            turned = psum.tile([P, passes, 2, P], F32, tag="turn")
-            for g in range(passes):
-                for u in range(2):
-                    nc.tensor.transpose(
-                        turned[:, g, u, :], words[:, WORDS * g + u : WORDS * (g + 1) : 2], ident[:]
-                    )
-            return turned
-
-        def quantise(t, first, passes, grouped):
-            chosen = slice(first, first + passes)
-            nc.vector.quantize_mx(
-                out=a_words[:, t, chosen, :].rearrange("p g r -> p (g r)").bitcast(FP8X4),
-                scales=a_scales[:, t, chosen, :].rearrange("p g r -> p (g r)"),
-                in_=grouped[:, chosen, :].rearrange("p g c -> p (g c)"),
-            )
-
-        def prepare(t):
-            x_turned = turn(x_sb[:, t, :].bitcast(F32), 1)
-            h_turned = turn(h_sb[:, t, :].bitcast(F32), 2)
-            grouped = stage.tile([P, A_PASSES, 4 * P], BF16, align_bytes=64)
-            word_halves = grouped[:].bitcast(F32).rearrange("p g (r u) -> p g r u", u=2)
-            nc.vector.tensor_copy(
-                out=word_halves[:, X_PASS : X_PASS + 1], in_=x_turned[:].rearrange("p g u r -> p g r u")
-            )
-            nc.scalar.copy(out=word_halves[:, H_PASS : H_PASS + 2], in_=h_turned[:].rearrange("p g u r -> p g r u"))
-            quantise(t, X_PASS, 1, grouped)
-            quantise(t, H_PASS, 2, grouped)
-
-        def mx_sum(acc, t, half, operands):
-            cols = slice(half * N_TILE, (half + 1) * N_TILE)
-            byte_cols = slice(half * 2 * N_TILE, (half + 1) * 2 * N_TILE)
-            for i, (a, w) in enumerate(operands):
-                nc.tensor.matmul_mx(
-                    out=acc[:],
-                    lhsT=a_words[:, t, a, :].bitcast(FP8X4),
-                    lhsT_scale=a_scales[:, t, a, :],
-                    rhs=w_words[:, w, byte_cols].bitcast(FP4X4),
-                    rhs_scale=w_scales[:, w, cols],
-                    start=(i == 0),
-                    stop=(i == len(operands) - 1),
+        def quantise(source, passes, copy_out, grouped, words, scales):
+            for first in range(0, TOKEN_TILES * passes, 2):
+                turned = psum.tile([P, 2, 2, P], F32, tag="bank")
+                for i in range(2):
+                    t, g = divmod(first + i, passes)
+                    pairs = source[:, t, :].bitcast(F32)
+                    for u in range(2):
+                        nc.tensor.transpose(
+                            turned[:, i, u, :], pairs[:, WORDS * g + u : WORDS * (g + 1) : 2], ident[:]
+                        )
+                both = slice(first, first + 2)
+                copy_out(
+                    out=grouped[:, both, :].bitcast(F32).rearrange("p i (r u) -> p i r u", u=2),
+                    in_=turned[:].rearrange("p i u r -> p i r u"),
+                )
+                nc.vector.quantize_mx(
+                    out=words[:, both, :].rearrange("p i r -> p (i r)").bitcast(FP8X4),
+                    scales=scales[:, both, :].rearrange("p i r -> p (i r)"),
+                    in_=grouped[:, both, :].rearrange("p i c -> p (i c)"),
                 )
 
-        def output_tile(t, half):
-            rows = slice(t * P, (t + 1) * P)
+        def mx_sum(acc, half, stationary, first):
             cols = slice(half * N_TILE, (half + 1) * N_TILE)
+            byte_cols = slice(half * 2 * N_TILE, (half + 1) * 2 * N_TILE)
+            for i, (words, scales) in enumerate(stationary):
+                nc.tensor.matmul_mx(
+                    out=acc[:],
+                    lhsT=words.bitcast(FP8X4),
+                    lhsT_scale=scales,
+                    rhs=w_words[:, first + i, byte_cols].bitcast(FP4X4),
+                    rhs_scale=w_scales[:, first + i, cols],
+                    start=(i == 0),
+                    stop=(i == len(stationary) - 1),
+                )
 
-            x_in_acc = psum.tile([P, N_TILE], F32, tag="x_in")
-            mx_sum(x_in_acc, t, half, [(X_PASS, W_IN)])
-            pre_acc = psum.tile([P, N_TILE], F32, tag="pre")
-            mx_sum(pre_acc, t, half, [(X_PASS, GATE), (H_PASS, GATE + 1), (H_PASS + 1, GATE + 2)])
-            rec_acc = psum.tile([P, N_TILE], F32, tag="rec")
-            mx_sum(rec_acc, t, half, [(H_PASS, W_REC), (H_PASS + 1, W_REC + 1)])
+        def quantised(t):
+            x_q = (x_words[:, t, :], x_scales[:, t, :])
+            h_q = [(h_words[:, 2 * t + g, :], h_scales[:, 2 * t + g, :]) for g in range(2)]
+            return x_q, h_q
 
-            x_in = work.tile([P, N_TILE], F32)
-            nc.scalar.copy(out=x_in[:], in_=x_in_acc[:])
-            nc.sync.dma_start(out=out_0[rows, cols], in_=x_in[:])
-
-            leak = ahead.tile([P, N_TILE], F32)
-            nc.gpsimd.tensor_tensor(out=leak[:], in0=h_sb[:, t, cols], in1=inv_tau_all[:, cols], op=ALU.mult)
-            base = work.tile([P, N_TILE], F32)
-            nc.gpsimd.tensor_tensor(out=base[:], in0=x_in[:], in1=leak[:], op=ALU.subtract)
-
+        def gate_of(t, half):
+            cols = slice(half * N_TILE, (half + 1) * N_TILE)
+            x_q, h_q = quantised(t)
+            pre_acc = psum.tile([P, N_TILE], F32, tag="bank")
+            mx_sum(pre_acc, half, [x_q] + h_q, GATE)
             pre = work.tile([P, N_TILE], F32)
             nc.vector.tensor_tensor(out=pre[:], in0=pre_acc[:], in1=bias_all[:, cols], op=ALU.add)
             squashed = work.tile([P, N_TILE], F32)
             nc.scalar.activation(out=squashed[:], in_=pre[:], func=ACT.Tanh)
             gate = work.tile([P, N_TILE], F32)
             nc.scalar.activation(out=gate[:], in_=squashed[:], func=ACT.Sigmoid)
+            return gate
+
+        def outputs_of(t, half, gate):
+            rows = slice(t * P, (t + 1) * P)
+            cols = slice(half * N_TILE, (half + 1) * N_TILE)
+            x_q, h_q = quantised(t)
+            x_in_acc = psum.tile([P, N_TILE], F32, tag="bank")
+            mx_sum(x_in_acc, half, [x_q], W_IN)
+            rec_acc = psum.tile([P, N_TILE], F32, tag="bank")
+            mx_sum(rec_acc, half, h_q, W_REC)
+
+            x_in = work.tile([P, N_TILE], F32)
+            nc.scalar.copy(out=x_in[:], in_=x_in_acc[:])
+            nc.sync.dma_start(out=out_0[rows, cols], in_=x_in[:])
+
+            base = work.tile([P, N_TILE], F32)
+            nc.vector.tensor_tensor(out=base[:], in0=x_in_acc[:], in1=leak[:, t, cols], op=ALU.subtract)
             gated = work.tile([P, N_TILE], F32)
             nc.vector.tensor_tensor(out=gated[:], in0=gate[:], in1=rec_acc[:], op=ALU.mult)
+            adder = nc.gpsimd if half == 0 else nc.vector
             k1 = work.tile([P, N_TILE], F32)
-            nc.vector.tensor_tensor(out=k1[:], in0=gated[:], in1=base[:], op=ALU.add)
+            adder.tensor_tensor(out=k1[:], in0=gated[:], in1=base[:], op=ALU.add)
             nc.sync.dma_start(out=out_1[rows, cols], in_=k1[:])
 
-        prepare(0)
         spread(bias_cols, bias_all)
         spread(inv_tau_cols, inv_tau_all)
+        quantise(x_sb, 1, nc.vector.tensor_copy, x_grouped, x_words, x_scales)
+        quantise(h_sb, 2, nc.scalar.copy, h_grouped, h_words, h_scales)
         for half in range(HALVES):
+            cols = slice(half * N_TILE, (half + 1) * N_TILE)
             for t in range(TOKEN_TILES):
-                if half == 0 and t + 1 < TOKEN_TILES:
-                    prepare(t + 1)
-                output_tile(t, half)
+                nc.gpsimd.tensor_tensor(
+                    out=leak[:, t, cols], in0=h_sb[:, t, cols], in1=inv_tau_all[:, cols], op=ALU.mult
+                )
+        tiles = [(t, half) for half in range(HALVES) for t in range(TOKEN_TILES)]
+        gate_ahead = gate_of(*tiles[0])
+        for i, (t, half) in enumerate(tiles):
+            gate = gate_ahead
+            if i + 1 < len(tiles):
+                gate_ahead = gate_of(*tiles[i + 1])
+            outputs_of(t, half, gate)

@@ -183,6 +183,9 @@ def tile_ltccell_pa_kernel(
             mx_sum(pre_acc, half, [x_q] + h_q, GATE)
             pre = work.tile([P, N_TILE], F32)
             nc.vector.tensor_tensor(out=pre[:], in0=pre_acc[:], in1=bias_all[:, cols], op=ALU.add)
+            if (t, half) == (0, 0):
+                warm = keep.tile([P, 1], F32)
+                nc.scalar.activation(out=warm[:], in_=pre[:, 0:1], func=ACT.Sigmoid)
             squashed = work.tile([P, N_TILE], F32)
             nc.scalar.activation(out=squashed[:], in_=pre[:], func=ACT.Tanh)
             gate = work.tile([P, N_TILE], F32)

@@ -136,8 +136,8 @@ def tile_ltccell_pa_kernel(
                     )
                 nc.vector.tensor_copy(out=everywhere[:, half * N_TILE : (half + 1) * N_TILE], in_=bank[:])
 
-        def quantise(source, passes, copy_out, grouped, words, scales):
-            for first in range(0, TOKEN_TILES * passes, 2):
+        def quantise(source, passes, copy_out, grouped, words, scales, banks):
+            for first in [2 * bank for bank in banks]:
                 turned = psum.tile([P, 2, 2, P], F32, tag="bank")
                 for i in range(2):
                     t, g = divmod(first + i, passes)
@@ -214,10 +214,11 @@ def tile_ltccell_pa_kernel(
             adder.tensor_tensor(out=k1[:], in0=gated[:], in1=base[:], op=ALU.add)
             nc.sync.dma_start(out=out_1[rows, cols], in_=k1[:])
 
+        quantise(x_sb, 1, nc.vector.tensor_copy, x_grouped, x_words, x_scales, (0, 1))
         spread(bias_cols, bias_all)
+        quantise(h_sb, 2, nc.scalar.copy, h_grouped, h_words, h_scales, (0, 1))
         spread(inv_tau_cols, inv_tau_all)
-        quantise(x_sb, 1, nc.vector.tensor_copy, x_grouped, x_words, x_scales)
-        quantise(h_sb, 2, nc.scalar.copy, h_grouped, h_words, h_scales)
+        quantise(h_sb, 2, nc.scalar.copy, h_grouped, h_words, h_scales, (2, 3))
         for half in range(HALVES):
             cols = slice(half * N_TILE, (half + 1) * N_TILE)
             for t in range(TOKEN_TILES):

@@ -48,7 +48,7 @@ def tile_ltccell_pa_kernel(
     nc = tc.nc
     with ExitStack() as ctx:
         keep = ctx.enter_context(tc.tile_pool(name="keep", bufs=1))
-        work = ctx.enter_context(tc.tile_pool(name="work", bufs=4))
+        work = ctx.enter_context(tc.tile_pool(name="work", bufs=6))
         psum = ctx.enter_context(tc.psum_pool(name="psum", bufs=8))
 
         ident = keep.tile([P, P], F32)
@@ -124,7 +124,7 @@ def tile_ltccell_pa_kernel(
         inv_tau_cols = keep.tile([P, CHUNKS], F32)
         nc.vector.reciprocal(out=inv_tau_cols[:], in_=tau_p[:])
 
-        def spread(one_to_a_partition, everywhere):
+        def spread(one_to_a_partition, everywhere, copy_out):
             for half in range(HALVES):
                 bank = psum.tile([P, N_TILE], F32, tag="bank")
                 for q in range(N_TILE // P):
@@ -134,7 +134,7 @@ def tile_ltccell_pa_kernel(
                         one_to_a_partition[:, j : j + 1].to_broadcast([P, P]),
                         ident[:],
                     )
-                nc.vector.tensor_copy(out=everywhere[:, half * N_TILE : (half + 1) * N_TILE], in_=bank[:])
+                copy_out(out=everywhere[:, half * N_TILE : (half + 1) * N_TILE], in_=bank[:])
 
         def quantise(source, passes, copy_out, grouped, words, scales, banks):
             for first in [2 * bank for bank in banks]:
@@ -209,15 +209,15 @@ def tile_ltccell_pa_kernel(
             nc.vector.tensor_tensor(out=base[:], in0=x_in_acc[:], in1=leak[:, t, cols], op=ALU.subtract)
             gated = work.tile([P, N_TILE], F32)
             nc.vector.tensor_tensor(out=gated[:], in0=gate[:], in1=rec_acc[:], op=ALU.mult)
-            adder = nc.gpsimd if half == 0 else nc.vector
+            adder = nc.vector if (half == HALVES - 1 and t >= TOKEN_TILES - 2) else nc.gpsimd
             k1 = work.tile([P, N_TILE], F32)
             adder.tensor_tensor(out=k1[:], in0=gated[:], in1=base[:], op=ALU.add)
             nc.sync.dma_start(out=out_1[rows, cols], in_=k1[:])
 
         quantise(x_sb, 1, nc.vector.tensor_copy, x_grouped, x_words, x_scales, (0, 1))
-        spread(bias_cols, bias_all)
+        spread(bias_cols, bias_all, nc.vector.tensor_copy)
         quantise(h_sb, 2, nc.scalar.copy, h_grouped, h_words, h_scales, (0, 1))
-        spread(inv_tau_cols, inv_tau_all)
+        spread(inv_tau_cols, inv_tau_all, nc.scalar.copy)
         quantise(h_sb, 2, nc.scalar.copy, h_grouped, h_words, h_scales, (2, 3))
         for half in range(HALVES):
             cols = slice(half * N_TILE, (half + 1) * N_TILE)

@@ -52,6 +52,7 @@ def tile_ltccell_pa_kernel(
         psum = ctx.enter_context(tc.psum_pool(name="psum", bufs=8))
 
         ident = keep.tile([P, P], F32)
+        ident_bf16 = keep.tile([P, P], BF16)
         vec_rows = keep.tile([P, P], BF16)
         x_sb = keep.tile([P, TOKEN_TILES, IN], BF16)
         h_sb = keep.tile([P, TOKEN_TILES, H], BF16)
@@ -69,6 +70,10 @@ def tile_ltccell_pa_kernel(
 
         make_identity(nc, ident[:])
         nc.vector.memset(vec_rows[:], 0.0)
+        one = keep.tile([P, 1], F32)
+        nc.vector.memset(one[:], 1.0)
+        warm = keep.tile([P, 2], F32)
+        nc.scalar.activation(out=warm[:, 0:1], in_=one[:], func=ACT.Sigmoid)
         nc.vector.memset(w_scales[:].bitcast(I32), 0)
 
         def load_scales(scales, first):
@@ -89,34 +94,35 @@ def tile_ltccell_pa_kernel(
 
         nc.sync.dma_start(out=vec_rows[0:CHUNKS, :], in_=tau.rearrange("(j c) -> j c", c=P))
         nc.sync.dma_start(out=vec_rows[CHUNKS : 2 * CHUNKS, :], in_=gate_b.rearrange("(j c) -> j c", c=P))
-        nc.sync.dma_start(out=x_sb[:], in_=x.rearrange("(t p) k -> p t k", p=P))
+        nc.sync.dma_start(out=x_sb[:, 0:2, :], in_=x[0 : 2 * P, :].rearrange("(t p) k -> p t k", p=P))
+        nc.sync.dma_start(out=x_sb[:, 2:4, :], in_=x[2 * P : 4 * P, :].rearrange("(t p) k -> p t k", p=P))
         nc.sync.dma_start(out=h_sb[:, 0:2, :], in_=h[0 : 2 * P, :].rearrange("(t p) k -> p t k", p=P))
-        nc.sync.dma_start(out=h_sb[:, 2:4, :], in_=h[2 * P : 4 * P, :].rearrange("(t p) k -> p t k", p=P))
         load_scales(gate_w_scales, GATE)
         load_scales(W_in_scales, W_IN)
         load_scales(W_rec_scales, W_REC)
-        for half in range(HALVES):
-            load_words(gate_w_words, GATE, half)
-            load_words(W_in_words, W_IN, half)
-            load_words(W_rec_words, W_REC, half)
+        load_words(gate_w_words, GATE, 0)
+        nc.sync.dma_start(out=h_sb[:, 2:4, :], in_=h[2 * P : 4 * P, :].rearrange("(t p) k -> p t k", p=P))
+        load_words(W_in_words, W_IN, 0)
+        load_words(W_rec_words, W_REC, 0)
+        load_words(gate_w_words, GATE, 1)
+        load_words(W_in_words, W_IN, 1)
+        load_words(W_rec_words, W_REC, 1)
 
-        vec_f32 = keep.tile([P, P], F32)
-        nc.vector.tensor_copy(out=vec_f32[:], in_=vec_rows[:])
-        vec_t = psum.tile([P, P], F32, tag="bank")
-        nc.tensor.transpose(vec_t[:], vec_f32[:], ident[:])
-        vec_cols = keep.tile([P, 2 * CHUNKS], F32)
-        nc.vector.tensor_copy(out=vec_cols[:], in_=vec_t[:, 0 : 2 * CHUNKS])
-        tau_cols = vec_cols[:, 0:CHUNKS]
-        bias_cols = vec_cols[:, CHUNKS : 2 * CHUNKS]
+        nc.vector.tensor_copy(out=ident_bf16[:], in_=ident[:])
+        vec_t = psum.tile([P, P], BF16, tag="bank")
+        nc.tensor.transpose(vec_t[:], vec_rows[:], ident_bf16[:])
 
         tau_abs = keep.tile([P, CHUNKS], F32)
-        nc.vector.scalar_tensor_tensor(
-            out=tau_abs[:], in0=tau_cols, scalar=-1.0, in1=tau_cols, op0=ALU.mult, op1=ALU.max
-        )
+        nc.scalar.activation(out=tau_abs[:], in_=vec_t[:, 0:CHUNKS], func=ACT.Abs)
         tau_sig = keep.tile([P, CHUNKS], F32)
         nc.scalar.activation(out=tau_sig[:], in_=tau_abs[:], func=ACT.Sigmoid)
         tau_log = keep.tile([P, CHUNKS], F32)
         nc.scalar.activation(out=tau_log[:], in_=tau_sig[:], func=ACT.Ln, scale=INV_E)
+        nc.scalar.activation(out=warm[:, 1:2], in_=tau_log[:, 0:1], func=ACT.Sigmoid)
+        vec_cols = keep.tile([P, 2 * CHUNKS], F32)
+        nc.vector.tensor_copy(out=vec_cols[:], in_=vec_t[:, 0 : 2 * CHUNKS])
+        tau_cols = vec_cols[:, 0:CHUNKS]
+        bias_cols = vec_cols[:, CHUNKS : 2 * CHUNKS]
         tau_p = keep.tile([P, CHUNKS], F32)
         nc.vector.scalar_tensor_tensor(
             out=tau_p[:], in0=tau_cols, scalar=0.0, in1=tau_log[:], op0=ALU.max, op1=ALU.subtract
@@ -183,9 +189,6 @@ def tile_ltccell_pa_kernel(
             mx_sum(pre_acc, half, [x_q] + h_q, GATE)
             pre = work.tile([P, N_TILE], F32)
             nc.vector.tensor_tensor(out=pre[:], in0=pre_acc[:], in1=bias_all[:, cols], op=ALU.add)
-            if (t, half) == (0, 0):
-                warm = keep.tile([P, 1], F32)
-                nc.scalar.activation(out=warm[:], in_=pre[:, 0:1], func=ACT.Sigmoid)
             squashed = work.tile([P, N_TILE], F32)
             nc.scalar.activation(out=squashed[:], in_=pre[:], func=ACT.Tanh)
             gate = work.tile([P, N_TILE], F32)

@@ -97,11 +97,11 @@ def tile_ltccell_pa_kernel(
         nc.sync.dma_start(out=x_sb[:, 0:2, :], in_=x[0 : 2 * P, :].rearrange("(t p) k -> p t k", p=P))
         nc.sync.dma_start(out=x_sb[:, 2:4, :], in_=x[2 * P : 4 * P, :].rearrange("(t p) k -> p t k", p=P))
         nc.sync.dma_start(out=h_sb[:, 0:2, :], in_=h[0 : 2 * P, :].rearrange("(t p) k -> p t k", p=P))
+        nc.sync.dma_start(out=h_sb[:, 2:4, :], in_=h[2 * P : 4 * P, :].rearrange("(t p) k -> p t k", p=P))
         load_scales(gate_w_scales, GATE)
         load_scales(W_in_scales, W_IN)
         load_scales(W_rec_scales, W_REC)
         load_words(gate_w_words, GATE, 0)
-        nc.sync.dma_start(out=h_sb[:, 2:4, :], in_=h[2 * P : 4 * P, :].rearrange("(t p) k -> p t k", p=P))
         load_words(W_in_words, W_IN, 0)
         load_words(W_rec_words, W_REC, 0)
         load_words(gate_w_words, GATE, 1)

@@ -51,6 +51,11 @@ def tile_ltccell_pa_kernel(
         work = ctx.enter_context(tc.tile_pool(name="work", bufs=6))
         psum = ctx.enter_context(tc.psum_pool(name="psum", bufs=8))
 
+        x_rows = x.rearrange("(p t) k -> p t k", t=TOKEN_TILES)
+        h_rows = h.rearrange("(p t) k -> p t k", t=TOKEN_TILES)
+        x_in_rows = out_0.rearrange("(p t) n -> p t n", t=TOKEN_TILES)
+        k1_rows = out_1.rearrange("(p t) n -> p t n", t=TOKEN_TILES)
+
         ident = keep.tile([P, P], F32)
         ident_bf16 = keep.tile([P, P], BF16)
         vec_rows = keep.tile([P, P], BF16)
@@ -94,10 +99,10 @@ def tile_ltccell_pa_kernel(
 
         nc.sync.dma_start(out=vec_rows[0:CHUNKS, :], in_=tau.rearrange("(j c) -> j c", c=P))
         nc.sync.dma_start(out=vec_rows[CHUNKS : 2 * CHUNKS, :], in_=gate_b.rearrange("(j c) -> j c", c=P))
-        nc.sync.dma_start(out=x_sb[:, 0:2, :], in_=x[0 : 2 * P, :].rearrange("(t p) k -> p t k", p=P))
-        nc.sync.dma_start(out=x_sb[:, 2:4, :], in_=x[2 * P : 4 * P, :].rearrange("(t p) k -> p t k", p=P))
-        nc.sync.dma_start(out=h_sb[:, 0:2, :], in_=h[0 : 2 * P, :].rearrange("(t p) k -> p t k", p=P))
-        nc.sync.dma_start(out=h_sb[:, 2:4, :], in_=h[2 * P : 4 * P, :].rearrange("(t p) k -> p t k", p=P))
+        nc.sync.dma_start(out=x_sb[:, 0:2, :], in_=x_rows[:, 0:2, :])
+        nc.sync.dma_start(out=x_sb[:, 2:4, :], in_=x_rows[:, 2:4, :])
+        nc.sync.dma_start(out=h_sb[:, 0:2, :], in_=h_rows[:, 0:2, :])
+        nc.sync.dma_start(out=h_sb[:, 2:4, :], in_=h_rows[:, 2:4, :])
         load_scales(gate_w_scales, GATE)
         load_scales(W_in_scales, W_IN)
         load_scales(W_rec_scales, W_REC)
@@ -196,7 +201,6 @@ def tile_ltccell_pa_kernel(
             return gate
 
         def outputs_of(t, half, gate):
-            rows = slice(t * P, (t + 1) * P)
             cols = slice(half * N_TILE, (half + 1) * N_TILE)
             x_q, h_q = quantised(t)
             x_in_acc = psum.tile([P, N_TILE], F32, tag="bank")
@@ -206,7 +210,7 @@ def tile_ltccell_pa_kernel(
 
             x_in = work.tile([P, N_TILE], F32)
             nc.scalar.copy(out=x_in[:], in_=x_in_acc[:])
-            nc.sync.dma_start(out=out_0[rows, cols], in_=x_in[:])
+            nc.sync.dma_start(out=x_in_rows[:, t, cols], in_=x_in[:])
 
             base = work.tile([P, N_TILE], F32)
             nc.vector.tensor_tensor(out=base[:], in0=x_in_acc[:], in1=leak[:, t, cols], op=ALU.subtract)
@@ -215,7 +219,7 @@ def tile_ltccell_pa_kernel(
             adder = nc.vector if (half == HALVES - 1 and t >= TOKEN_TILES - 2) else nc.gpsimd
             k1 = work.tile([P, N_TILE], F32)
             adder.tensor_tensor(out=k1[:], in0=gated[:], in1=base[:], op=ALU.add)
-            nc.sync.dma_start(out=out_1[rows, cols], in_=k1[:])
+            nc.sync.dma_start(out=k1_rows[:, t, cols], in_=k1[:])
 
         quantise(x_sb, 1, nc.vector.tensor_copy, x_grouped, x_words, x_scales, (0, 1))
         spread(bias_cols, bias_all, nc.vector.tensor_copy)

@@ -200,14 +200,16 @@ def tile_ltccell_pa_kernel(
             nc.scalar.activation(out=gate[:], in_=squashed[:], func=ACT.Sigmoid)
             return gate
 
-        def outputs_of(t, half, gate):
-            cols = slice(half * N_TILE, (half + 1) * N_TILE)
+        def products_of(t, half):
             x_q, h_q = quantised(t)
             x_in_acc = psum.tile([P, N_TILE], F32, tag="bank")
             mx_sum(x_in_acc, half, [x_q], W_IN)
             rec_acc = psum.tile([P, N_TILE], F32, tag="bank")
             mx_sum(rec_acc, half, h_q, W_REC)
+            return x_in_acc, rec_acc
 
+        def outputs_of(t, half, gate, x_in_acc, rec_acc):
+            cols = slice(half * N_TILE, (half + 1) * N_TILE)
             x_in = work.tile([P, N_TILE], F32)
             nc.scalar.copy(out=x_in[:], in_=x_in_acc[:])
             nc.sync.dma_start(out=x_in_rows[:, t, cols], in_=x_in[:])
@@ -236,6 +238,7 @@ def tile_ltccell_pa_kernel(
         gate_ahead = gate_of(*tiles[0])
         for i, (t, half) in enumerate(tiles):
             gate = gate_ahead
+            x_in_acc, rec_acc = products_of(t, half)
             if i + 1 < len(tiles):
                 gate_ahead = gate_of(*tiles[i + 1])
-            outputs_of(t, half, gate)
+            outputs_of(t, half, gate, x_in_acc, rec_acc)

from contextlib import ExitStack

import concourse.mybir as mybir
from concourse.masks import make_identity

F32 = mybir.dt.float32
BF16 = mybir.dt.bfloat16
U8 = mybir.dt.uint8
U32 = mybir.dt.uint32
I32 = mybir.dt.int32
FP8X4 = mybir.dt.float8_e4m3fn_x4
FP4X4 = mybir.dt.float4_e2m1fn_x4
ACT = mybir.ActivationFunctionType
ALU = mybir.AluOpType

P = 128
B, IN, H = 512, 512, 1024
K_PASS = 512
WORDS = K_PASS // 2
N_TILE = 512
TOKEN_TILES = B // P
HALVES = H // N_TILE
CHUNKS = H // P

W_IN, GATE, W_REC = 0, 1, 4
W_PASSES = 6

INV_E = 0.36787944117144233

FLOPS = 2 * B * H * (IN + (IN + H) + H)


def tile_ltccell_pa_kernel(
    tc,
    x,
    h,
    tau,
    W_in_words,
    W_in_scales,
    W_rec_words,
    W_rec_scales,
    gate_w_words,
    gate_w_scales,
    gate_b,
    out_0,
    out_1,
):
    nc = tc.nc
    with ExitStack() as ctx:
        keep = ctx.enter_context(tc.tile_pool(name="keep", bufs=1))
        work = ctx.enter_context(tc.tile_pool(name="work", bufs=6))
        psum = ctx.enter_context(tc.psum_pool(name="psum", bufs=8))

        x_rows = x.rearrange("(p t) k -> p t k", t=TOKEN_TILES)
        h_rows = h.rearrange("(p t) k -> p t k", t=TOKEN_TILES)
        x_in_rows = out_0.rearrange("(p t) n -> p t n", t=TOKEN_TILES)
        k1_rows = out_1.rearrange("(p t) n -> p t n", t=TOKEN_TILES)

        ident = keep.tile([P, P], F32)
        ident_bf16 = keep.tile([P, P], BF16)
        vec_rows = keep.tile([P, P], BF16)
        x_sb = keep.tile([P, TOKEN_TILES, IN], BF16)
        h_sb = keep.tile([P, TOKEN_TILES, H], BF16)
        w_words = keep.tile([P, W_PASSES, 2 * H], U8, align_bytes=64)
        w_scales = keep.tile([P, W_PASSES, H], U8, align_bytes=64)
        x_grouped = keep.tile([P, TOKEN_TILES, 4 * P], BF16, align_bytes=64)
        x_words = keep.tile([P, TOKEN_TILES, P], U32, align_bytes=64)
        x_scales = keep.tile([P, TOKEN_TILES, P], U8, align_bytes=64)
        h_grouped = keep.tile([P, 2 * TOKEN_TILES, 4 * P], BF16, align_bytes=64)
        h_words = keep.tile([P, 2 * TOKEN_TILES, P], U32, align_bytes=64)
        h_scales = keep.tile([P, 2 * TOKEN_TILES, P], U8, align_bytes=64)
        bias_all = keep.tile([P, H], F32)
        inv_tau_all = keep.tile([P, H], F32)
        leak = keep.tile([P, TOKEN_TILES, H], F32)

        make_identity(nc, ident[:])
        nc.vector.memset(vec_rows[:], 0.0)
        one = keep.tile([P, 1], F32)
        nc.vector.memset(one[:], 1.0)
        warm = keep.tile([P, 2], F32)
        nc.scalar.activation(out=warm[:, 0:1], in_=one[:], func=ACT.Sigmoid)
        nc.vector.memset(w_scales[:].bitcast(I32), 0)

        def load_scales(scales, first):
            passes = scales.shape[0]
            for r in range(4):
                nc.sync.dma_start(
                    out=w_scales[r:P:32, first : first + passes, :].bitcast(I32),
                    in_=scales[:, r:16:4, :].rearrange("g q n -> q g n").bitcast(I32),
                )

        def load_words(words, first, half):
            passes = words.shape[0]
            byte_cols = slice(half * 2 * N_TILE, (half + 1) * 2 * N_TILE)
            nc.sync.dma_start(
                out=w_words[:, first : first + passes, byte_cols].bitcast(I32),
                in_=words[:, :, byte_cols].rearrange("g p b -> p g b").bitcast(I32),
            )

        nc.sync.dma_start(out=vec_rows[0:CHUNKS, :], in_=tau.rearrange("(j c) -> j c", c=P))
        nc.sync.dma_start(out=vec_rows[CHUNKS : 2 * CHUNKS, :], in_=gate_b.rearrange("(j c) -> j c", c=P))
        nc.sync.dma_start(out=x_sb[:, 0:2, :], in_=x_rows[:, 0:2, :])
        nc.sync.dma_start(out=x_sb[:, 2:4, :], in_=x_rows[:, 2:4, :])
        nc.sync.dma_start(out=h_sb[:, 0:2, :], in_=h_rows[:, 0:2, :])
        nc.sync.dma_start(out=h_sb[:, 2:4, :], in_=h_rows[:, 2:4, :])
        load_scales(gate_w_scales, GATE)
        load_scales(W_in_scales, W_IN)
        load_scales(W_rec_scales, W_REC)
        load_words(gate_w_words, GATE, 0)
        load_words(W_in_words, W_IN, 0)
        load_words(W_rec_words, W_REC, 0)
        load_words(gate_w_words, GATE, 1)
        load_words(W_in_words, W_IN, 1)
        load_words(W_rec_words, W_REC, 1)

        nc.vector.tensor_copy(out=ident_bf16[:], in_=ident[:])
        vec_t = psum.tile([P, P], BF16, tag="bank")
        nc.tensor.transpose(vec_t[:], vec_rows[:], ident_bf16[:])

        tau_abs = keep.tile([P, CHUNKS], F32)
        nc.scalar.activation(out=tau_abs[:], in_=vec_t[:, 0:CHUNKS], func=ACT.Abs)
        tau_sig = keep.tile([P, CHUNKS], F32)
        nc.scalar.activation(out=tau_sig[:], in_=tau_abs[:], func=ACT.Sigmoid)
        tau_log = keep.tile([P, CHUNKS], F32)
        nc.scalar.activation(out=tau_log[:], in_=tau_sig[:], func=ACT.Ln, scale=INV_E)
        nc.scalar.activation(out=warm[:, 1:2], in_=tau_log[:, 0:1], func=ACT.Sigmoid)
        vec_cols = keep.tile([P, 2 * CHUNKS], F32)
        nc.vector.tensor_copy(out=vec_cols[:], in_=vec_t[:, 0 : 2 * CHUNKS])
        tau_cols = vec_cols[:, 0:CHUNKS]
        bias_cols = vec_cols[:, CHUNKS : 2 * CHUNKS]
        tau_p = keep.tile([P, CHUNKS], F32)
        nc.vector.scalar_tensor_tensor(
            out=tau_p[:], in0=tau_cols, scalar=0.0, in1=tau_log[:], op0=ALU.max, op1=ALU.subtract
        )
        inv_tau_cols = keep.tile([P, CHUNKS], F32)
        nc.vector.reciprocal(out=inv_tau_cols[:], in_=tau_p[:])

        def spread(one_to_a_partition, everywhere, copy_out):
            for half in range(HALVES):
                bank = psum.tile([P, N_TILE], F32, tag="bank")
                for q in range(N_TILE // P):
                    j = half * (N_TILE // P) + q
                    nc.tensor.transpose(
                        bank[:, q * P : (q + 1) * P],
                        one_to_a_partition[:, j : j + 1].to_broadcast([P, P]),
                        ident[:],
                    )
                copy_out(out=everywhere[:, half * N_TILE : (half + 1) * N_TILE], in_=bank[:])

        def quantise(source, passes, copy_out, grouped, words, scales, banks):
            for first in [2 * bank for bank in banks]:
                turned = psum.tile([P, 2, 2, P], F32, tag="bank")
                for i in range(2):
                    t, g = divmod(first + i, passes)
                    pairs = source[:, t, :].bitcast(F32)
                    for u in range(2):
                        nc.tensor.transpose(
                            turned[:, i, u, :], pairs[:, WORDS * g + u : WORDS * (g + 1) : 2], ident[:]
                        )
                both = slice(first, first + 2)
                copy_out(
                    out=grouped[:, both, :].bitcast(F32).rearrange("p i (r u) -> p i r u", u=2),
                    in_=turned[:].rearrange("p i u r -> p i r u"),
                )
                nc.vector.quantize_mx(
                    out=words[:, both, :].rearrange("p i r -> p (i r)").bitcast(FP8X4),
                    scales=scales[:, both, :].rearrange("p i r -> p (i r)"),
                    in_=grouped[:, both, :].rearrange("p i c -> p (i c)"),
                )

        def mx_sum(acc, half, stationary, first):
            cols = slice(half * N_TILE, (half + 1) * N_TILE)
            byte_cols = slice(half * 2 * N_TILE, (half + 1) * 2 * N_TILE)
            for i, (words, scales) in enumerate(stationary):
                nc.tensor.matmul_mx(
                    out=acc[:],
                    lhsT=words.bitcast(FP8X4),
                    lhsT_scale=scales,
                    rhs=w_words[:, first + i, byte_cols].bitcast(FP4X4),
                    rhs_scale=w_scales[:, first + i, cols],
                    start=(i == 0),
                    stop=(i == len(stationary) - 1),
                )

        def quantised(t):
            x_q = (x_words[:, t, :], x_scales[:, t, :])
            h_q = [(h_words[:, 2 * t + g, :], h_scales[:, 2 * t + g, :]) for g in range(2)]
            return x_q, h_q

        def gate_of(t, half):
            cols = slice(half * N_TILE, (half + 1) * N_TILE)
            x_q, h_q = quantised(t)
            pre_acc = psum.tile([P, N_TILE], F32, tag="bank")
            mx_sum(pre_acc, half, [x_q] + h_q, GATE)
            pre = work.tile([P, N_TILE], F32)
            nc.vector.tensor_tensor(out=pre[:], in0=pre_acc[:], in1=bias_all[:, cols], op=ALU.add)
            squashed = work.tile([P, N_TILE], F32)
            nc.scalar.activation(out=squashed[:], in_=pre[:], func=ACT.Tanh)
            gate = work.tile([P, N_TILE], F32)
            nc.scalar.activation(out=gate[:], in_=squashed[:], func=ACT.Sigmoid)
            return gate

        def products_of(t, half):
            x_q, h_q = quantised(t)
            x_in_acc = psum.tile([P, N_TILE], F32, tag="bank")
            mx_sum(x_in_acc, half, [x_q], W_IN)
            rec_acc = psum.tile([P, N_TILE], F32, tag="bank")
            mx_sum(rec_acc, half, h_q, W_REC)
            return x_in_acc, rec_acc

        def outputs_of(t, half, gate, x_in_acc, rec_acc):
            cols = slice(half * N_TILE, (half + 1) * N_TILE)
            x_in = work.tile([P, N_TILE], F32)
            nc.scalar.copy(out=x_in[:], in_=x_in_acc[:])
            nc.sync.dma_start(out=x_in_rows[:, t, cols], in_=x_in[:])

            base = work.tile([P, N_TILE], F32)
            nc.vector.tensor_tensor(out=base[:], in0=x_in_acc[:], in1=leak[:, t, cols], op=ALU.subtract)
            gated = work.tile([P, N_TILE], F32)
            nc.vector.tensor_tensor(out=gated[:], in0=gate[:], in1=rec_acc[:], op=ALU.mult)
            adder = nc.vector if (half == HALVES - 1 and t >= TOKEN_TILES - 2) else nc.gpsimd
            k1 = work.tile([P, N_TILE], F32)
            adder.tensor_tensor(out=k1[:], in0=gated[:], in1=base[:], op=ALU.add)
            nc.sync.dma_start(out=k1_rows[:, t, cols], in_=k1[:])

        quantise(x_sb, 1, nc.vector.tensor_copy, x_grouped, x_words, x_scales, (0, 1))
        spread(bias_cols, bias_all, nc.vector.tensor_copy)
        quantise(h_sb, 2, nc.scalar.copy, h_grouped, h_words, h_scales, (0, 1))
        spread(inv_tau_cols, inv_tau_all, nc.scalar.copy)
        quantise(h_sb, 2, nc.scalar.copy, h_grouped, h_words, h_scales, (2, 3))
        for half in range(HALVES):
            cols = slice(half * N_TILE, (half + 1) * N_TILE)
            for t in range(TOKEN_TILES):
                nc.gpsimd.tensor_tensor(
                    out=leak[:, t, cols], in0=h_sb[:, t, cols], in1=inv_tau_all[:, cols], op=ALU.mult
                )
        tiles = [(t, half) for half in range(HALVES) for t in range(TOKEN_TILES)]
        gate_ahead = gate_of(*tiles[0])
        for i, (t, half) in enumerate(tiles):
            gate = gate_ahead
            x_in_acc, rec_acc = products_of(t, half)
            if i + 1 < len(tiles):
                gate_ahead = gate_of(*tiles[i + 1])
            outputs_of(t, half, gate, x_in_acc, rec_acc)
